import numpy as np
import ml_dtypes


def mxq(x, axis, fmt="e4m3"):
    dtype, down = {"e4m3": (ml_dtypes.float8_e4m3fn, 7), "e5m2": (ml_dtypes.float8_e5m2, 14)}[fmt]
    v = np.moveaxis(np.asarray(x, np.float32).astype(ml_dtypes.bfloat16).astype(np.float64), axis, -1)
    blocks = v.reshape(v.shape[:-1] + (-1, 32))
    amax = np.abs(blocks).max(-1, keepdims=True)
    byte = np.maximum(np.where(amax > 0, np.frexp(amax)[1] - 1 + 127, 0) - down, 1)
    scale = np.exp2(byte - 127.0)
    codes = (blocks / scale).astype(np.float32).astype(dtype).astype(np.float64)
    return np.moveaxis((codes * scale).reshape(v.shape), -1, axis)


WIDE = False


def mx_kscale(k):
    if not WIDE:
        return np.ones(k)
    levels = np.array([10, -10, 5, -5, 0])
    a = np.random.permutation(np.resize(levels, k // 512 * 4)).reshape(k // 512, 4)
    idx = np.arange(k)
    return np.exp2(a[idx // 512, idx % 128 // 32])


BF16 = ml_dtypes.bfloat16


def bf(x):
    return np.asarray(x, np.float32).astype(BF16)


def f64(x):
    return np.asarray(x).astype(np.float64)


E2M1 = np.array([0.0, 0.5, 1.0, 1.5, 2.0, 3.0, 4.0, 6.0, -0.0, -0.5, -1.0, -1.5, -2.0, -3.0, -4.0, -6.0])


def pack_weight(w, fmt):
    k, n = w.shape
    w = f64(bf(w)).reshape(k // 32, 32, n)
    amax = np.abs(w).max(1)
    if fmt == "e4m3":
        byte = np.frexp(amax)[1] - 1 + 127 - 7
    else:
        mant, ex = np.frexp(amax / 6.0)
        byte = np.where(mant > 0.5, ex, ex - 1) + 127
    byte = np.clip(np.where(amax > 0, byte, 1), 1, 254)
    scaled = (w * np.exp2(127.0 - byte)[:, None, :]).reshape(k, n).astype(np.float32)
    by_word = np.ascontiguousarray(scaled.reshape(k // 512, 128, 4, n).transpose(0, 1, 3, 2))
    if fmt == "e4m3":
        words = by_word.astype(ml_dtypes.float8_e4m3fn).view(np.uint8)
    else:
        c = by_word.astype(ml_dtypes.float4_e2m1fn).view(np.uint8) & 0xF
        words = c[..., 0::2] | (c[..., 1::2] << 4)
    return np.ascontiguousarray(words), np.ascontiguousarray(byte.astype(np.uint8).reshape(k // 512, 16, n))


def unpack_weight(words, scales, fmt):
    g, p, n, _ = words.shape
    if fmt == "e4m3":
        vals = np.ascontiguousarray(words).view(ml_dtypes.float8_e4m3fn).astype(np.float64)
    else:
        nib = np.empty((g, p, n, 4), np.uint8)
        nib[..., 0::2] = words & 0xF
        nib[..., 1::2] = words >> 4
        vals = E2M1[nib]
    vals = vals * np.repeat(np.exp2(scales.astype(np.float64) - 127.0), 8, axis=1)[..., None]
    return vals.transpose(0, 1, 3, 2).reshape(g * 512, n)

def pack4(w):
    words, scales = pack_weight(w, "e2m1")
    return words.reshape(words.shape[0], 128, -1), scales


def unpack4(words, scales):
    return unpack_weight(words.reshape(words.shape[0], 128, -1, 2), scales, "e2m1")


B, NB, NL, NG, NK = 4096, 512, 1536, 500, 3
N2 = 2 * NB


def setup_inputs():
    s = mx_kscale(N2)
    r = s[:NB]
    Volt = bf(np.random.standard_normal((B, N2)) * s)
    y = np.random.standard_normal((NB, N2)) * 4.0 / np.sqrt(N2) / s[None, :] / r[:, None]
    yc = np.random.standard_normal((NB, N2)) * 4.0 / np.sqrt(N2) / s[None, :] / r[:, None]
    PQ_Loads = bf(np.random.standard_normal((B, N2)))
    PQ_Gens = bf(np.random.standard_normal((B, N2)))
    y_words, y_scales = pack4(np.ascontiguousarray(y.T))
    yc_words, yc_scales = pack4(np.ascontiguousarray(yc.T))
    return {'Volt': Volt,
            'Y_top_words': y_words,
            'Y_top_scales': y_scales,
            'Yconj_top_words': yc_words,
            'Yconj_top_scales': yc_scales,
            'PQ_Loads': PQ_Loads,
            'PQ_Gens': PQ_Gens}


def reference(Volt, Y_top_words, Y_top_scales, Yconj_top_words, Yconj_top_scales, PQ_Loads, PQ_Gens):
    V = f64(Volt)
    Vq = mxq(V, 1, 'e4m3')
    YV = Vq @ unpack4(Y_top_words, Y_top_scales)
    YcV = Vq @ unpack4(Yconj_top_words, Yconj_top_scales)
    out = np.sum(V[:, :NB] * YV, axis=1) + np.sum(V[:, :NB] * YcV, axis=1)
    pq = f64(PQ_Loads) - f64(PQ_Gens)
    return out + np.sum(pq[:, :NB], axis=1) + np.sum(pq[:, NB:], axis=1)

@@ -1,0 +1,227 @@
+from contextlib import ExitStack
+
+import concourse.mybir as mybir
+from concourse.masks import make_identity
+
+FLOPS = 2 * 2 * 4096 * 1024 * 512
+
+BF16 = mybir.dt.bfloat16
+F32 = mybir.dt.float32
+I32 = mybir.dt.int32
+U32 = mybir.dt.uint32
+U8 = mybir.dt.uint8
+FP8X4 = mybir.dt.float8_e4m3fn_x4
+FP4X4 = mybir.dt.float4_e2m1fn_x4
+MULT = mybir.AluOpType.mult
+ADD = mybir.AluOpType.add
+SUBTRACT = mybir.AluOpType.subtract
+COPY = mybir.ActivationFunctionType.Copy
+
+P = 128
+BATCH = 4096
+K = 1024
+NB = 512
+K_PASS = 512
+GROUPS = K // K_PASS
+WEIGHTS = 2
+TILES = BATCH // P
+CHUNK_TILES = 4
+CHUNKS = TILES // CHUNK_TILES
+ROUND_TILES = 4
+ROUNDS = TILES // ROUND_TILES
+HALF_ROUND = ROUND_TILES // 2
+LOADS_AHEAD = 3
+
+
+def tile_kktloss_pc_t_kernel(
+    tc, Volt, Y_top_words, Y_top_scales, Yconj_top_words, Yconj_top_scales, PQ_Loads, PQ_Gens, out
+):
+    nc = tc.nc
+
+    volt_rows = Volt.rearrange("(p t) k -> p t k", t=TILES)
+    loads_rows = PQ_Loads.rearrange("(p t) k -> p t k", t=TILES)
+    gens_rows = PQ_Gens.rearrange("(p t) k -> p t k", t=TILES)
+    out_rows = out.rearrange("(p t) -> p t", t=TILES)
+
+    with ExitStack() as stack:
+        const = stack.enter_context(tc.tile_pool(name="const", bufs=1))
+        volt_pool = stack.enter_context(tc.tile_pool(name="volt", bufs=CHUNKS))
+        pq_pool = stack.enter_context(tc.tile_pool(name="pq", bufs=LOADS_AHEAD + 1))
+        grouped_pool = stack.enter_context(tc.tile_pool(name="grouped", bufs=ROUND_TILES))
+        codes_pool = stack.enter_context(tc.tile_pool(name="codes", bufs=2 * ROUND_TILES))
+        unread_pool = stack.enter_context(tc.tile_pool(name="unread", bufs=3))
+        turned_pool = stack.enter_context(tc.psum_pool(name="turned", bufs=4))
+        acc_pool = stack.enter_context(tc.psum_pool(name="acc", bufs=4))
+        stack.enter_context(tc.manual_schedule())
+
+        identity = const.tile([P, P], F32)
+        make_identity(nc, identity[:])
+
+        w_words = const.tile([P, WEIGHTS, GROUPS, 2 * NB], U8, align_bytes=64)
+        w_planes = const.tile([P, WEIGHTS, GROUPS, NB], U8, align_bytes=64)
+        nc.vector.memset(w_planes[:].rearrange("p w g n -> p (w g n)").bitcast(I32), 0)
+
+        dots = const.tile([P, TILES], F32)
+        balance = const.tile([P, TILES], F32)
+        load_sums = const.tile([P, TILES // 2], F32)
+        gen_sums = const.tile([P, TILES // 2], F32)
+        total = const.tile([P, TILES], F32)
+
+        volt = {}
+        loads = {}
+        gens = {}
+        turned = {}
+        grouped = {}
+        codes = {}
+        code_scales = {}
+        acc = {}
+
+        def load_volt(c):
+            chunk = volt_pool.tile([P, CHUNK_TILES, K], BF16, name="volt_chunk")
+            nc.sync.dma_start(out=chunk[:], in_=volt_rows[:, c * CHUNK_TILES : (c + 1) * CHUNK_TILES, :])
+            volt[c] = chunk
+
+        def load_pq(c):
+            loads_chunk = pq_pool.tile([P, CHUNK_TILES, K], BF16, name="loads_chunk")
+            nc.sync.dma_start(out=loads_chunk[:], in_=loads_rows[:, c * CHUNK_TILES : (c + 1) * CHUNK_TILES, :])
+            loads[c] = loads_chunk
+            gens_chunk = pq_pool.tile([P, CHUNK_TILES, K], BF16, name="gens_chunk")
+            nc.sync.dma_start(out=gens_chunk[:], in_=gens_rows[:, c * CHUNK_TILES : (c + 1) * CHUNK_TILES, :])
+            gens[c] = gens_chunk
+
+        def load_scales(w, scales):
+            by_row = scales.bitcast(I32).rearrange("g (q r) n -> r q g n", r=4)
+            for r in range(4):
+                nc.sync.dma_start(out=w_planes[r:P:32, w].bitcast(I32), in_=by_row[r])
+
+        def load_words(w, words):
+            nc.sync.dma_start(out=w_words[:, w].bitcast(I32), in_=words.bitcast(I32).rearrange("g p n -> p g n"))
+
+        def row_tile(chunks, i):
+            return chunks[i // CHUNK_TILES][:, i % CHUNK_TILES, :]
+
+        def transpose(i):
+            words = row_tile(volt, i).bitcast(F32)
+            bank = turned_pool.tile([P, GROUPS, 2, P], F32, name="turned_bank")
+            for g in range(GROUPS):
+                for u in range(2):
+                    nc.tensor.transpose(bank[:, g, u, :], words[:, 256 * g + u : 256 * (g + 1) : 2], identity[:])
+            turned[i] = bank
+
+        def regroup(i):
+            side_by_side = grouped_pool.tile([P, K], BF16, name="side_by_side", align_bytes=64)
+            nc.scalar.copy(
+                out=side_by_side[:].bitcast(F32).rearrange("p (g b u) -> p g b u", g=GROUPS, u=2),
+                in_=turned[i][:].rearrange("p g u b -> p g b u"),
+            )
+            grouped[i] = side_by_side
+
+        def quantise(i):
+            packed = codes_pool.tile([P, GROUPS, P], U32, name="packed", align_bytes=64)
+            plane = codes_pool.tile([P, GROUPS, P], U8, name="plane", align_bytes=64)
+            nc.vector.quantize_mx(
+                out=packed[:].rearrange("p g b -> p (g b)").bitcast(FP8X4),
+                scales=plane[:].rearrange("p g b -> p (g b)"),
+                in_=grouped[i][:],
+            )
+            codes[i] = packed
+            code_scales[i] = plane
+
+        def multiply(i):
+            bank = acc_pool.tile([P, NB], F32, name="acc_bank")
+            for g in range(GROUPS):
+                for w in range(WEIGHTS):
+                    nc.tensor.matmul_mx(
+                        out=bank[:],
+                        lhsT=codes[i][:, g, :].bitcast(FP8X4),
+                        lhsT_scale=code_scales[i][:, g, :],
+                        rhs=w_words[:, w, g, :].bitcast(FP4X4),
+                        rhs_scale=w_planes[:, w, g, :],
+                        start=(g == 0 and w == 0),
+                        stop=(g == GROUPS - 1 and w == WEIGHTS - 1),
+                    )
+            acc[i] = bank
+
+        def dot(i):
+            products = unread_pool.tile([P, NB], F32, name="products")
+            nc.vector.scalar_tensor_tensor(
+                out=products[:],
+                in0=acc[i][:],
+                scalar=1.0,
+                in1=row_tile(volt, i)[:, 0:NB],
+                op0=MULT,
+                op1=MULT,
+                accum_out=dots[:, i : i + 1],
+            )
+
+        def balance_on_vector(i):
+            differences = unread_pool.tile([P, K], F32, name="differences")
+            nc.vector.scalar_tensor_tensor(
+                out=differences[:],
+                in0=row_tile(loads, i),
+                scalar=1.0,
+                in1=row_tile(gens, i),
+                op0=MULT,
+                op1=SUBTRACT,
+                accum_out=balance[:, i : i + 1],
+            )
+
+        def sum_on_scalar(chunks, i, sign, sums):
+            copied = unread_pool.tile([P, K], BF16, name="copied")
+            nc.scalar.activation(
+                out=copied[:], in_=row_tile(chunks, i), func=COPY, scale=sign, accum_out=sums[:, i // 2 : i // 2 + 1]
+            )
+
+        load_volt(0)
+        load_scales(0, Y_top_scales)
+        load_pq(0)
+        load_words(0, Y_top_words)
+        load_scales(1, Yconj_top_scales)
+        load_words(1, Yconj_top_words)
+        for c in range(1, LOADS_AHEAD):
+            load_volt(c)
+            load_pq(c)
+
+        for i in range(ROUND_TILES):
+            transpose(i)
+        for i in range(ROUND_TILES):
+            regroup(i)
+            quantise(i)
+
+        for r in range(ROUNDS):
+            first = r * ROUND_TILES
+            following = first + ROUND_TILES
+            c = r + LOADS_AHEAD
+            if c < CHUNKS:
+                load_volt(c)
+                load_pq(c)
+
+            for i in range(first, first + HALF_ROUND):
+                multiply(i)
+            if following < TILES:
+                for i in range(following, following + ROUND_TILES):
+                    transpose(i)
+            for i in range(first + HALF_ROUND, following):
+                multiply(i)
+
+            for h in range(HALF_ROUND):
+                sum_on_scalar(loads, first + 2 * h + 1, 1.0, load_sums)
+            if following < TILES:
+                for i in range(following, following + ROUND_TILES):
+                    regroup(i)
+            for h in range(HALF_ROUND):
+                sum_on_scalar(gens, first + 2 * h + 1, -1.0, gen_sums)
+
+            for h in range(HALF_ROUND):
+                balance_on_vector(first + 2 * h)
+                dot(first + h)
+            if following < TILES:
+                for i in range(following, following + ROUND_TILES):
+                    quantise(i)
+            for i in range(first + HALF_ROUND, following):
+                dot(i)
+
+        odd_columns = balance[:].rearrange("p (h two) -> p h two", two=2)[:, :, 1]
+        nc.vector.tensor_tensor(out=odd_columns, in0=load_sums[:], in1=gen_sums[:], op=ADD)
+        nc.vector.tensor_tensor(out=total[:], in0=dots[:], in1=balance[:], op=ADD)
+        nc.sync.dma_start(out=out_rows, in_=total[:])

@@ -25,11 +25,10 @@ K_PASS = 512
 GROUPS = K // K_PASS
 WEIGHTS = 2
 TILES = BATCH // P
-CHUNK_TILES = 4
-CHUNKS = TILES // CHUNK_TILES
 ROUND_TILES = 4
 ROUNDS = TILES // ROUND_TILES
 HALF_ROUND = ROUND_TILES // 2
+ROUNDS_AHEAD = 2
 LOADS_AHEAD = 3
 
 
@@ -45,10 +44,10 @@ def tile_kktloss_pc_t_kernel(
 
     with ExitStack() as stack:
         const = stack.enter_context(tc.tile_pool(name="const", bufs=1))
-        volt_pool = stack.enter_context(tc.tile_pool(name="volt", bufs=CHUNKS))
-        pq_pool = stack.enter_context(tc.tile_pool(name="pq", bufs=LOADS_AHEAD + 1))
+        volt_pool = stack.enter_context(tc.tile_pool(name="volt", bufs=2 * ROUNDS))
+        pq_pool = stack.enter_context(tc.tile_pool(name="pq", bufs=2 * (LOADS_AHEAD + 1)))
         grouped_pool = stack.enter_context(tc.tile_pool(name="grouped", bufs=ROUND_TILES))
-        codes_pool = stack.enter_context(tc.tile_pool(name="codes", bufs=2 * ROUND_TILES))
+        codes_pool = stack.enter_context(tc.tile_pool(name="codes", bufs=(ROUNDS_AHEAD + 1) * ROUND_TILES))
         unread_pool = stack.enter_context(tc.tile_pool(name="unread", bufs=3))
         turned_pool = stack.enter_context(tc.psum_pool(name="turned", bufs=4))
         acc_pool = stack.enter_context(tc.psum_pool(name="acc", bufs=4))
@@ -76,18 +75,22 @@ def tile_kktloss_pc_t_kernel(
         code_scales = {}
         acc = {}
 
-        def load_volt(c):
-            chunk = volt_pool.tile([P, CHUNK_TILES, K], BF16, name="volt_chunk")
-            nc.sync.dma_start(out=chunk[:], in_=volt_rows[:, c * CHUNK_TILES : (c + 1) * CHUNK_TILES, :])
-            volt[c] = chunk
+        def load_half(held, pool, name, rows, h):
+            half = pool.tile([P, HALF_ROUND, K], BF16, name=name)
+            nc.sync.dma_start(out=half[:], in_=rows[:, h * HALF_ROUND : (h + 1) * HALF_ROUND, :])
+            held[h] = half
 
-        def load_pq(c):
-            loads_chunk = pq_pool.tile([P, CHUNK_TILES, K], BF16, name="loads_chunk")
-            nc.sync.dma_start(out=loads_chunk[:], in_=loads_rows[:, c * CHUNK_TILES : (c + 1) * CHUNK_TILES, :])
-            loads[c] = loads_chunk
-            gens_chunk = pq_pool.tile([P, CHUNK_TILES, K], BF16, name="gens_chunk")
-            nc.sync.dma_start(out=gens_chunk[:], in_=gens_rows[:, c * CHUNK_TILES : (c + 1) * CHUNK_TILES, :])
-            gens[c] = gens_chunk
+        def load_volt(r):
+            load_half(volt, volt_pool, "volt_half", volt_rows, 2 * r)
+            load_half(volt, volt_pool, "volt_half", volt_rows, 2 * r + 1)
+
+        def load_step(r):
+            load_half(loads, pq_pool, "loads_half", loads_rows, 2 * r)
+            if r + ROUNDS_AHEAD < ROUNDS:
+                load_volt(r + ROUNDS_AHEAD)
+            load_half(gens, pq_pool, "gens_half", gens_rows, 2 * r)
+            load_half(loads, pq_pool, "loads_half", loads_rows, 2 * r + 1)
+            load_half(gens, pq_pool, "gens_half", gens_rows, 2 * r + 1)
 
         def load_scales(w, scales):
             by_row = scales.bitcast(I32).rearrange("g (q r) n -> r q g n", r=4)
@@ -97,8 +100,8 @@ def tile_kktloss_pc_t_kernel(
         def load_words(w, words):
             nc.sync.dma_start(out=w_words[:, w].bitcast(I32), in_=words.bitcast(I32).rearrange("g p n -> p g n"))
 
-        def row_tile(chunks, i):
-            return chunks[i // CHUNK_TILES][:, i % CHUNK_TILES, :]
+        def row_tile(held, i):
+            return held[i // HALF_ROUND][:, i % HALF_ROUND, :]
 
         def transpose(i):
             words = row_tile(volt, i).bitcast(F32)
@@ -108,9 +111,9 @@ def tile_kktloss_pc_t_kernel(
                     nc.tensor.transpose(bank[:, g, u, :], words[:, 256 * g + u : 256 * (g + 1) : 2], identity[:])
             turned[i] = bank
 
-        def regroup(i):
+        def regroup(i, copy):
             side_by_side = grouped_pool.tile([P, K], BF16, name="side_by_side", align_bytes=64)
-            nc.scalar.copy(
+            copy(
                 out=side_by_side[:].bitcast(F32).rearrange("p (g b u) -> p g b u", g=GROUPS, u=2),
                 in_=turned[i][:].rearrange("p g u b -> p g b u"),
             )
@@ -172,53 +175,66 @@ def tile_kktloss_pc_t_kernel(
                 out=copied[:], in_=row_tile(chunks, i), func=COPY, scale=sign, accum_out=sums[:, i // 2 : i // 2 + 1]
             )
 
-        load_volt(0)
+        def prepare_on_tensor(first):
+            for i in range(first, first + ROUND_TILES):
+                transpose(i)
+
+        def prepare_on_scalar(first):
+            for i in range(first, first + ROUND_TILES - 1):
+                regroup(i, nc.scalar.copy)
+
+        def prepare_on_vector(first):
+            for i in range(first, first + ROUND_TILES - 1):
+                quantise(i)
+            regroup(first + ROUND_TILES - 1, nc.vector.tensor_copy)
+
+        load_half(volt, volt_pool, "volt_half", volt_rows, 0)
         load_scales(0, Y_top_scales)
-        load_pq(0)
+        load_half(volt, volt_pool, "volt_half", volt_rows, 1)
         load_words(0, Y_top_words)
+        load_volt(1)
         load_scales(1, Yconj_top_scales)
         load_words(1, Yconj_top_words)
-        for c in range(1, LOADS_AHEAD):
-            load_volt(c)
-            load_pq(c)
+        for r in range(LOADS_AHEAD):
+            load_step(r)
 
-        for i in range(ROUND_TILES):
-            transpose(i)
-        for i in range(ROUND_TILES):
-            regroup(i)
-            quantise(i)
+        for r in range(ROUNDS_AHEAD):
+            prepare_on_tensor(r * ROUND_TILES)
+            prepare_on_scalar(r * ROUND_TILES)
+            prepare_on_vector(r * ROUND_TILES)
+            quantise((r + 1) * ROUND_TILES - 1)
 
         for r in range(ROUNDS):
             first = r * ROUND_TILES
-            following = first + ROUND_TILES
-            c = r + LOADS_AHEAD
-            if c < CHUNKS:
-                load_volt(c)
-                load_pq(c)
+            middle = first + HALF_ROUND
+            end = first + ROUND_TILES
+            ahead = first + ROUNDS_AHEAD * ROUND_TILES
+            if r + LOADS_AHEAD < ROUNDS:
+                load_step(r + LOADS_AHEAD)
 
-            for i in range(first, first + HALF_ROUND):
+            for i in range(first, middle):
                 multiply(i)
-            if following < TILES:
-                for i in range(following, following + ROUND_TILES):
-                    transpose(i)
-            for i in range(first + HALF_ROUND, following):
+            if ahead < TILES:
+                prepare_on_tensor(ahead)
+            for i in range(middle, end):
                 multiply(i)
 
-            for h in range(HALF_ROUND):
-                sum_on_scalar(loads, first + 2 * h + 1, 1.0, load_sums)
-            if following < TILES:
-                for i in range(following, following + ROUND_TILES):
-                    regroup(i)
-            for h in range(HALF_ROUND):
-                sum_on_scalar(gens, first + 2 * h + 1, -1.0, gen_sums)
+            sum_on_scalar(loads, first + 1, 1.0, load_sums)
+            sum_on_scalar(gens, first + 1, -1.0, gen_sums)
+            if ahead < TILES:
+                prepare_on_scalar(ahead)
+            sum_on_scalar(loads, middle + 1, 1.0, load_sums)
+            sum_on_scalar(gens, middle + 1, -1.0, gen_sums)
 
-            for h in range(HALF_ROUND):
-                balance_on_vector(first + 2 * h)
-                dot(first + h)
-            if following < TILES:
-                for i in range(following, following + ROUND_TILES):
-                    quantise(i)
-            for i in range(first + HALF_ROUND, following):
+            balance_on_vector(first)
+            for i in range(first, middle):
+                dot(i)
+            if ahead < TILES:
+                prepare_on_vector(ahead)
+            balance_on_vector(middle)
+            if ahead < TILES:
+                quantise(ahead + ROUND_TILES - 1)
+            for i in range(middle, end):
                 dot(i)
 
         odd_columns = balance[:].rearrange("p (h two) -> p h two", two=2)[:, :, 1]

@@ -25,11 +25,13 @@ K_PASS = 512
 GROUPS = K // K_PASS
 WEIGHTS = 2
 TILES = BATCH // P
+CHUNK_TILES = 4
+CHUNKS = TILES // CHUNK_TILES
 ROUND_TILES = 4
 ROUNDS = TILES // ROUND_TILES
 HALF_ROUND = ROUND_TILES // 2
-ROUNDS_AHEAD = 2
-LOADS_AHEAD = 3
+LOADS_AHEAD = 2
+PQ_BUFS = 4
 
 
 def tile_kktloss_pc_t_kernel(
@@ -44,10 +46,10 @@ def tile_kktloss_pc_t_kernel(
 
     with ExitStack() as stack:
         const = stack.enter_context(tc.tile_pool(name="const", bufs=1))
-        volt_pool = stack.enter_context(tc.tile_pool(name="volt", bufs=2 * ROUNDS))
-        pq_pool = stack.enter_context(tc.tile_pool(name="pq", bufs=2 * (LOADS_AHEAD + 1)))
+        volt_pool = stack.enter_context(tc.tile_pool(name="volt", bufs=CHUNKS))
+        pq_pool = stack.enter_context(tc.tile_pool(name="pq", bufs=PQ_BUFS))
         grouped_pool = stack.enter_context(tc.tile_pool(name="grouped", bufs=ROUND_TILES))
-        codes_pool = stack.enter_context(tc.tile_pool(name="codes", bufs=(ROUNDS_AHEAD + 1) * ROUND_TILES))
+        codes_pool = stack.enter_context(tc.tile_pool(name="codes", bufs=2 * ROUND_TILES))
         unread_pool = stack.enter_context(tc.tile_pool(name="unread", bufs=3))
         turned_pool = stack.enter_context(tc.psum_pool(name="turned", bufs=4))
         acc_pool = stack.enter_context(tc.psum_pool(name="acc", bufs=4))
@@ -75,22 +77,17 @@ def tile_kktloss_pc_t_kernel(
         code_scales = {}
         acc = {}
 
-        def load_half(held, pool, name, rows, h):
-            half = pool.tile([P, HALF_ROUND, K], BF16, name=name)
-            nc.sync.dma_start(out=half[:], in_=rows[:, h * HALF_ROUND : (h + 1) * HALF_ROUND, :])
-            held[h] = half
+        def load_chunk(held, pool, name, rows, c):
+            chunk = pool.tile([P, CHUNK_TILES, K], BF16, name=name)
+            nc.sync.dma_start(out=chunk[:], in_=rows[:, c * CHUNK_TILES : (c + 1) * CHUNK_TILES, :])
+            held[c] = chunk
 
-        def load_volt(r):
-            load_half(volt, volt_pool, "volt_half", volt_rows, 2 * r)
-            load_half(volt, volt_pool, "volt_half", volt_rows, 2 * r + 1)
-
-        def load_step(r):
-            load_half(loads, pq_pool, "loads_half", loads_rows, 2 * r)
-            if r + ROUNDS_AHEAD < ROUNDS:
-                load_volt(r + ROUNDS_AHEAD)
-            load_half(gens, pq_pool, "gens_half", gens_rows, 2 * r)
-            load_half(loads, pq_pool, "loads_half", loads_rows, 2 * r + 1)
-            load_half(gens, pq_pool, "gens_half", gens_rows, 2 * r + 1)
+        def load_step(c):
+            if c + 1 < CHUNKS:
+                load_chunk(volt, volt_pool, "volt_chunk", volt_rows, c + 1)
+            load_chunk(gens, pq_pool, "gens_chunk", gens_rows, c)
+            if c + 1 < CHUNKS:
+                load_chunk(loads, pq_pool, "loads_chunk", loads_rows, c + 1)
 
         def load_scales(w, scales):
             by_row = scales.bitcast(I32).rearrange("g (q r) n -> r q g n", r=4)
@@ -100,8 +97,8 @@ def tile_kktloss_pc_t_kernel(
         def load_words(w, words):
             nc.sync.dma_start(out=w_words[:, w].bitcast(I32), in_=words.bitcast(I32).rearrange("g p n -> p g n"))
 
-        def row_tile(held, i):
-            return held[i // HALF_ROUND][:, i % HALF_ROUND, :]
+        def row_tile(chunks, i):
+            return chunks[i // CHUNK_TILES][:, i % CHUNK_TILES, :]
 
         def transpose(i):
             words = row_tile(volt, i).bitcast(F32)
@@ -111,9 +108,9 @@ def tile_kktloss_pc_t_kernel(
                     nc.tensor.transpose(bank[:, g, u, :], words[:, 256 * g + u : 256 * (g + 1) : 2], identity[:])
             turned[i] = bank
 
-        def regroup(i, copy):
+        def regroup(i):
             side_by_side = grouped_pool.tile([P, K], BF16, name="side_by_side", align_bytes=64)
-            copy(
+            nc.scalar.copy(
                 out=side_by_side[:].bitcast(F32).rearrange("p (g b u) -> p g b u", g=GROUPS, u=2),
                 in_=turned[i][:].rearrange("p g u b -> p g b u"),
             )
@@ -175,66 +172,52 @@ def tile_kktloss_pc_t_kernel(
                 out=copied[:], in_=row_tile(chunks, i), func=COPY, scale=sign, accum_out=sums[:, i // 2 : i // 2 + 1]
             )
 
-        def prepare_on_tensor(first):
-            for i in range(first, first + ROUND_TILES):
-                transpose(i)
-
-        def prepare_on_scalar(first):
-            for i in range(first, first + ROUND_TILES - 1):
-                regroup(i, nc.scalar.copy)
-
-        def prepare_on_vector(first):
-            for i in range(first, first + ROUND_TILES - 1):
-                quantise(i)
-            regroup(first + ROUND_TILES - 1, nc.vector.tensor_copy)
-
-        load_half(volt, volt_pool, "volt_half", volt_rows, 0)
+        load_chunk(volt, volt_pool, "volt_chunk", volt_rows, 0)
         load_scales(0, Y_top_scales)
-        load_half(volt, volt_pool, "volt_half", volt_rows, 1)
         load_words(0, Y_top_words)
-        load_volt(1)
+        load_chunk(loads, pq_pool, "loads_chunk", loads_rows, 0)
         load_scales(1, Yconj_top_scales)
         load_words(1, Yconj_top_words)
-        for r in range(LOADS_AHEAD):
-            load_step(r)
+        for c in range(LOADS_AHEAD):
+            load_step(c)
 
-        for r in range(ROUNDS_AHEAD):
-            prepare_on_tensor(r * ROUND_TILES)
-            prepare_on_scalar(r * ROUND_TILES)
-            prepare_on_vector(r * ROUND_TILES)
-            quantise((r + 1) * ROUND_TILES - 1)
+        for i in range(ROUND_TILES):
+            transpose(i)
+        for i in range(ROUND_TILES):
+            regroup(i)
+            quantise(i)
 
         for r in range(ROUNDS):
             first = r * ROUND_TILES
             middle = first + HALF_ROUND
-            end = first + ROUND_TILES
-            ahead = first + ROUNDS_AHEAD * ROUND_TILES
-            if r + LOADS_AHEAD < ROUNDS:
+            following = first + ROUND_TILES
+            prepared = range(following, min(following + ROUND_TILES, TILES))
+            if r + LOADS_AHEAD < CHUNKS:
                 load_step(r + LOADS_AHEAD)
 
             for i in range(first, middle):
                 multiply(i)
-            if ahead < TILES:
-                prepare_on_tensor(ahead)
-            for i in range(middle, end):
+            for i in prepared:
+                transpose(i)
+            for i in range(middle, following):
                 multiply(i)
 
-            sum_on_scalar(loads, first + 1, 1.0, load_sums)
-            sum_on_scalar(gens, first + 1, -1.0, gen_sums)
-            if ahead < TILES:
-                prepare_on_scalar(ahead)
-            sum_on_scalar(loads, middle + 1, 1.0, load_sums)
-            sum_on_scalar(gens, middle + 1, -1.0, gen_sums)
+            for i in range(first + 1, following, 2):
+                sum_on_scalar(loads, i, 1.0, load_sums)
+            for i in prepared:
+                regroup(i)
+            for i in range(first + 1, following, 2):
+                sum_on_scalar(gens, i, -1.0, gen_sums)
 
-            balance_on_vector(first)
             for i in range(first, middle):
                 dot(i)
-            if ahead < TILES:
-                prepare_on_vector(ahead)
+            balance_on_vector(first)
+            for i in prepared[:-1]:
+                quantise(i)
             balance_on_vector(middle)
-            if ahead < TILES:
-                quantise(ahead + ROUND_TILES - 1)
-            for i in range(middle, end):
+            for i in prepared[-1:]:
+                quantise(i)
+            for i in range(middle, following):
                 dot(i)
 
         odd_columns = balance[:].rearrange("p (h two) -> p h two", two=2)[:, :, 1]

@@ -77,15 +77,18 @@ def tile_kktloss_pc_t_kernel(
         code_scales = {}
         acc = {}
 
-        def load_chunk(held, pool, name, rows, c):
+        def load_chunk(held, pool, name, rows, c, pieces=1):
             chunk = pool.tile([P, CHUNK_TILES, K], BF16, name=name)
-            nc.sync.dma_start(out=chunk[:], in_=rows[:, c * CHUNK_TILES : (c + 1) * CHUNK_TILES, :])
+            step = CHUNK_TILES // pieces
+            for s in range(0, CHUNK_TILES, step):
+                first = c * CHUNK_TILES + s
+                nc.sync.dma_start(out=chunk[:, s : s + step, :], in_=rows[:, first : first + step, :])
             held[c] = chunk
 
         def load_step(c):
             if c + 1 < CHUNKS:
                 load_chunk(volt, volt_pool, "volt_chunk", volt_rows, c + 1)
-            load_chunk(gens, pq_pool, "gens_chunk", gens_rows, c)
+            load_chunk(gens, pq_pool, "gens_chunk", gens_rows, c, pieces=2 if c == CHUNKS - 1 else 1)
             if c + 1 < CHUNKS:
                 load_chunk(loads, pq_pool, "loads_chunk", loads_rows, c + 1)
 
@@ -209,16 +212,23 @@ def tile_kktloss_pc_t_kernel(
             for i in range(first + 1, following, 2):
                 sum_on_scalar(gens, i, -1.0, gen_sums)
 
-            for i in range(first, middle):
-                dot(i)
-            balance_on_vector(first)
-            for i in prepared[:-1]:
-                quantise(i)
-            balance_on_vector(middle)
-            for i in prepared[-1:]:
-                quantise(i)
-            for i in range(middle, following):
-                dot(i)
+            if r == ROUNDS - 1:
+                balance_on_vector(first)
+                dot(first)
+                balance_on_vector(middle)
+                for i in range(first + 1, following):
+                    dot(i)
+            else:
+                for i in range(first, middle):
+                    dot(i)
+                balance_on_vector(first)
+                for i in prepared[:-1]:
+                    quantise(i)
+                balance_on_vector(middle)
+                for i in prepared[-1:]:
+                    quantise(i)
+                for i in range(middle, following):
+                    dot(i)
 
         odd_columns = balance[:].rearrange("p (h two) -> p h two", two=2)[:, :, 1]
         nc.vector.tensor_tensor(out=odd_columns, in0=load_sums[:], in1=gen_sums[:], op=ADD)

@@ -64,13 +64,14 @@ def tile_kktloss_pc_t_kernel(
 
         dots = const.tile([P, TILES], F32)
         balance = const.tile([P, TILES], F32)
-        load_sums = const.tile([P, TILES // 2], F32)
-        gen_sums = const.tile([P, TILES // 2], F32)
+        second = const.tile([P, TILES], F32)
+        nc.gpsimd.memset(second[:], 0.0)
         total = const.tile([P, TILES], F32)
 
         volt = {}
         loads = {}
         gens = {}
+        gap = const.tile([P, K], F32)
         turned = {}
         grouped = {}
         codes = {}
@@ -172,8 +173,33 @@ def tile_kktloss_pc_t_kernel(
         def sum_on_scalar(chunks, i, sign, sums):
             copied = unread_pool.tile([P, K], BF16, name="copied")
             nc.scalar.activation(
-                out=copied[:], in_=row_tile(chunks, i), func=COPY, scale=sign, accum_out=sums[:, i // 2 : i // 2 + 1]
+                out=copied[:], in_=row_tile(chunks, i), func=COPY, scale=sign, accum_out=sums[:, i : i + 1]
             )
+
+        def gens_on_vector(i):
+            negated = unread_pool.tile([P, K], BF16, name="negated")
+            nc.vector.tensor_scalar(
+                out=negated[:],
+                in0=row_tile(gens, i),
+                scalar1=-1.0,
+                scalar2=None,
+                op0=MULT,
+                op1=ADD,
+                accum_out=second[:, i : i + 1],
+            )
+
+        def subtract_on_gpsimd(i):
+            for h in range(0, K, K // 2):
+                nc.gpsimd.tensor_tensor(
+                    out=gap[:, h : h + K // 2],
+                    in0=row_tile(loads, i)[:, h : h + K // 2],
+                    in1=row_tile(gens, i)[:, h : h + K // 2],
+                    op=SUBTRACT,
+                )
+
+        def gap_on_scalar(i):
+            copied = unread_pool.tile([P, K], BF16, name="copied")
+            nc.scalar.activation(out=copied[:], in_=gap[:], func=COPY, accum_out=balance[:, i : i + 1])
 
         load_chunk(volt, volt_pool, "volt_chunk", volt_rows, 0)
         load_scales(0, Y_top_scales)
@@ -205,18 +231,24 @@ def tile_kktloss_pc_t_kernel(
             for i in range(middle, following):
                 multiply(i)
 
-            for i in range(first + 1, following, 2):
-                sum_on_scalar(loads, i, 1.0, load_sums)
+            last = r == ROUNDS - 1
+            if last:
+                subtract_on_gpsimd(first)
+            for i in range(first + 1, following, 1 if last else 2):
+                sum_on_scalar(loads, i, 1.0, balance)
             for i in prepared:
                 regroup(i)
-            for i in range(first + 1, following, 2):
-                sum_on_scalar(gens, i, -1.0, gen_sums)
+            for i in range(first + 1, middle if last else following, 2):
+                sum_on_scalar(gens, i, -1.0, second)
+            if last:
+                gap_on_scalar(first)
 
-            if r == ROUNDS - 1:
-                balance_on_vector(first)
-                dot(first)
-                balance_on_vector(middle)
-                for i in range(first + 1, following):
+            if last:
+                for i in range(first, middle):
+                    dot(i)
+                for i in range(middle, following):
+                    gens_on_vector(i)
+                for i in range(middle, following):
                     dot(i)
             else:
                 for i in range(first, middle):
@@ -230,7 +262,6 @@ def tile_kktloss_pc_t_kernel(
                 for i in range(middle, following):
                     dot(i)
 
-        odd_columns = balance[:].rearrange("p (h two) -> p h two", two=2)[:, :, 1]
-        nc.vector.tensor_tensor(out=odd_columns, in0=load_sums[:], in1=gen_sums[:], op=ADD)
+        nc.vector.tensor_tensor(out=balance[:], in0=balance[:], in1=second[:], op=ADD)
         nc.vector.tensor_tensor(out=total[:], in0=dots[:], in1=balance[:], op=ADD)
         nc.sync.dma_start(out=out_rows, in_=total[:])

@@ -25,13 +25,13 @@ K_PASS = 512
 GROUPS = K // K_PASS
 WEIGHTS = 2
 TILES = BATCH // P
-CHUNK_TILES = 4
-CHUNKS = TILES // CHUNK_TILES
 ROUND_TILES = 4
 ROUNDS = TILES // ROUND_TILES
-HALF_ROUND = ROUND_TILES // 2
 LOADS_AHEAD = 2
-PQ_BUFS = 4
+VOLT_AHEAD = 2
+PQ_BUFS = 5
+
+BALANCE = ["VSVS"] * (ROUNDS - 1) + ["GSXX"]
 
 
 def tile_kktloss_pc_t_kernel(
@@ -46,10 +46,11 @@ def tile_kktloss_pc_t_kernel(
 
     with ExitStack() as stack:
         const = stack.enter_context(tc.tile_pool(name="const", bufs=1))
-        volt_pool = stack.enter_context(tc.tile_pool(name="volt", bufs=CHUNKS))
+        volt_pool = stack.enter_context(tc.tile_pool(name="volt", bufs=ROUNDS))
         pq_pool = stack.enter_context(tc.tile_pool(name="pq", bufs=PQ_BUFS))
-        grouped_pool = stack.enter_context(tc.tile_pool(name="grouped", bufs=ROUND_TILES))
-        codes_pool = stack.enter_context(tc.tile_pool(name="codes", bufs=2 * ROUND_TILES))
+        grouped_pool = stack.enter_context(tc.tile_pool(name="grouped", bufs=2 * ROUND_TILES))
+        codes_pool = stack.enter_context(tc.tile_pool(name="codes", bufs=3 * ROUND_TILES))
+        difference_pool = stack.enter_context(tc.tile_pool(name="difference", bufs=2))
         unread_pool = stack.enter_context(tc.tile_pool(name="unread", bufs=3))
         turned_pool = stack.enter_context(tc.psum_pool(name="turned", bufs=4))
         acc_pool = stack.enter_context(tc.psum_pool(name="acc", bufs=4))
@@ -64,34 +65,36 @@ def tile_kktloss_pc_t_kernel(
 
         dots = const.tile([P, TILES], F32)
         balance = const.tile([P, TILES], F32)
-        second = const.tile([P, TILES], F32)
-        nc.gpsimd.memset(second[:], 0.0)
+        gen_sums = const.tile([P, TILES], F32)
+        nc.gpsimd.memset(gen_sums[:], 0.0)
         total = const.tile([P, TILES], F32)
 
         volt = {}
         loads = {}
         gens = {}
-        gap = const.tile([P, K], F32)
         turned = {}
         grouped = {}
+        subtracted = {}
         codes = {}
         code_scales = {}
         acc = {}
 
         def load_chunk(held, pool, name, rows, c, pieces=1):
-            chunk = pool.tile([P, CHUNK_TILES, K], BF16, name=name)
-            step = CHUNK_TILES // pieces
-            for s in range(0, CHUNK_TILES, step):
-                first = c * CHUNK_TILES + s
+            chunk = pool.tile([P, ROUND_TILES, K], BF16, name=name)
+            step = ROUND_TILES // pieces
+            for s in range(0, ROUND_TILES, step):
+                first = c * ROUND_TILES + s
                 nc.sync.dma_start(out=chunk[:, s : s + step, :], in_=rows[:, first : first + step, :])
             held[c] = chunk
 
         def load_step(c):
-            if c + 1 < CHUNKS:
-                load_chunk(volt, volt_pool, "volt_chunk", volt_rows, c + 1)
-            load_chunk(gens, pq_pool, "gens_chunk", gens_rows, c, pieces=2 if c == CHUNKS - 1 else 1)
-            if c + 1 < CHUNKS:
-                load_chunk(loads, pq_pool, "loads_chunk", loads_rows, c + 1)
+            load_chunk(gens, pq_pool, "gens_chunk", gens_rows, c, pieces=2 if c == ROUNDS - 1 else 1)
+            if c + VOLT_AHEAD < ROUNDS:
+                load_chunk(volt, volt_pool, "volt_chunk", volt_rows, c + VOLT_AHEAD)
+            if c + 1 < ROUNDS:
+                load_chunk(
+                    loads, pq_pool, "loads_chunk", loads_rows, c + 1, pieces=1
+                )
 
         def load_scales(w, scales):
             by_row = scales.bitcast(I32).rearrange("g (q r) n -> r q g n", r=4)
@@ -102,7 +105,7 @@ def tile_kktloss_pc_t_kernel(
             nc.sync.dma_start(out=w_words[:, w].bitcast(I32), in_=words.bitcast(I32).rearrange("g p n -> p g n"))
 
         def row_tile(chunks, i):
-            return chunks[i // CHUNK_TILES][:, i % CHUNK_TILES, :]
+            return chunks[i // ROUND_TILES][:, i % ROUND_TILES, :]
 
         def transpose(i):
             words = row_tile(volt, i).bitcast(F32)
@@ -185,83 +188,78 @@ def tile_kktloss_pc_t_kernel(
                 scalar2=None,
                 op0=MULT,
                 op1=ADD,
-                accum_out=second[:, i : i + 1],
+                accum_out=gen_sums[:, i : i + 1],
             )
 
         def subtract_on_gpsimd(i):
+            difference = difference_pool.tile([P, K], F32, name="difference")
             for h in range(0, K, K // 2):
+                half = slice(h, h + K // 2)
                 nc.gpsimd.tensor_tensor(
-                    out=gap[:, h : h + K // 2],
-                    in0=row_tile(loads, i)[:, h : h + K // 2],
-                    in1=row_tile(gens, i)[:, h : h + K // 2],
-                    op=SUBTRACT,
+                    out=difference[:, half], in0=row_tile(loads, i)[:, half], in1=row_tile(gens, i)[:, half], op=SUBTRACT
                 )
+            subtracted[i] = difference
 
-        def gap_on_scalar(i):
+        def difference_on_scalar(i):
             copied = unread_pool.tile([P, K], BF16, name="copied")
-            nc.scalar.activation(out=copied[:], in_=gap[:], func=COPY, accum_out=balance[:, i : i + 1])
+            nc.scalar.activation(out=copied[:], in_=subtracted[i][:], func=COPY, accum_out=balance[:, i : i + 1])
 
         load_chunk(volt, volt_pool, "volt_chunk", volt_rows, 0)
         load_scales(0, Y_top_scales)
         load_words(0, Y_top_words)
-        load_chunk(loads, pq_pool, "loads_chunk", loads_rows, 0)
+        load_chunk(volt, volt_pool, "volt_chunk", volt_rows, 1)
         load_scales(1, Yconj_top_scales)
         load_words(1, Yconj_top_words)
+        load_chunk(loads, pq_pool, "loads_chunk", loads_rows, 0)
         for c in range(LOADS_AHEAD):
             load_step(c)
 
-        for i in range(ROUND_TILES):
+        for i in range(VOLT_AHEAD * ROUND_TILES):
             transpose(i)
-        for i in range(ROUND_TILES):
             regroup(i)
             quantise(i)
 
         for r in range(ROUNDS):
-            first = r * ROUND_TILES
-            middle = first + HALF_ROUND
-            following = first + ROUND_TILES
-            prepared = range(following, min(following + ROUND_TILES, TILES))
-            if r + LOADS_AHEAD < CHUNKS:
+            tiles = range(r * ROUND_TILES, (r + 1) * ROUND_TILES)
+            ahead = (r + VOLT_AHEAD) * ROUND_TILES
+            prepared = range(min(ahead, TILES), min(ahead + ROUND_TILES, TILES))
+            by = {who: [i for i, w in zip(tiles, BALANCE[r]) if w == who] for who in "VSXG"}
+            if r + LOADS_AHEAD < ROUNDS:
                 load_step(r + LOADS_AHEAD)
 
-            for i in range(first, middle):
+            for i in tiles:
                 multiply(i)
             for i in prepared:
                 transpose(i)
-            for i in range(middle, following):
-                multiply(i)
 
-            last = r == ROUNDS - 1
-            if last:
-                subtract_on_gpsimd(first)
-            for i in range(first + 1, following, 1 if last else 2):
-                sum_on_scalar(loads, i, 1.0, balance)
+            for i in by["G"]:
+                subtract_on_gpsimd(i)
+
+            for i in tiles:
+                if i in by["S"] or i in by["X"]:
+                    sum_on_scalar(loads, i, 1.0, balance)
+            for i in by["S"]:
+                sum_on_scalar(gens, i, -1.0, gen_sums)
+            for i in by["G"]:
+                difference_on_scalar(i)
             for i in prepared:
                 regroup(i)
-            for i in range(first + 1, middle if last else following, 2):
-                sum_on_scalar(gens, i, -1.0, second)
-            if last:
-                gap_on_scalar(first)
 
-            if last:
-                for i in range(first, middle):
-                    dot(i)
-                for i in range(middle, following):
-                    gens_on_vector(i)
-                for i in range(middle, following):
+            sums = [(balance_on_vector, i) for i in by["V"]] + [(gens_on_vector, i) for i in by["X"]]
+            if r == ROUNDS - 1:
+                for work, i in sums:
+                    work(i)
+                for i in tiles:
                     dot(i)
             else:
-                for i in range(first, middle):
+                for j, i in enumerate(tiles):
                     dot(i)
-                balance_on_vector(first)
-                for i in prepared[:-1]:
-                    quantise(i)
-                balance_on_vector(middle)
-                for i in prepared[-1:]:
-                    quantise(i)
-                for i in range(middle, following):
-                    dot(i)
+                    if j == 0:
+                        for work, tile in sums:
+                            work(tile)
+            for i in prepared:
+                quantise(i)
 
-        nc.vector.tensor_tensor(out=balance[:], in0=balance[:], in1=second[:], op=ADD)
+        nc.vector.tensor_tensor(out=balance[:], in0=balance[:], in1=gen_sums[:], op=ADD)
         nc.vector.tensor_tensor(out=total[:], in0=dots[:], in1=balance[:], op=ADD)
         nc.sync.dma_start(out=out_rows, in_=total[:])

@@ -162,7 +162,7 @@ def tile_kktloss_pc_t_kernel(
             )
 
         def balance_on_vector(i):
-            differences = unread_pool.tile([P, K], F32, name="differences")
+            differences = unread_pool.tile([P, K], BF16, name="differences")
             nc.vector.scalar_tensor_tensor(
                 out=differences[:],
                 in0=row_tile(loads, i),

@@ -31,7 +31,7 @@ LOADS_AHEAD = 2
 VOLT_AHEAD = 2
 PQ_BUFS = 5
 
-BALANCE = ["VSVS"] * (ROUNDS - 1) + ["GSXX"]
+BALANCE = ["VSVS"] * (ROUNDS - 2) + ["TSTS", "SGTG"]
 
 
 def tile_kktloss_pc_t_kernel(
@@ -63,11 +63,13 @@ def tile_kktloss_pc_t_kernel(
         w_planes = const.tile([P, WEIGHTS, GROUPS, NB], U8, align_bytes=64)
         nc.vector.memset(w_planes[:].rearrange("p w g n -> p (w g n)").bitcast(I32), 0)
 
-        dots = const.tile([P, TILES], F32)
-        balance = const.tile([P, TILES], F32)
-        gen_sums = const.tile([P, TILES], F32)
-        nc.gpsimd.memset(gen_sums[:], 0.0)
+        parts = const.tile([P, 3, TILES], F32)
+        dots = parts[:, 0, :]
+        balance = parts[:, 1, :]
+        gen_sums = parts[:, 2, :]
+        nc.gpsimd.memset(gen_sums, 0.0)
         total = const.tile([P, TILES], F32)
+        seen = const.tile([P, 1], U32)
 
         volt = {}
         loads = {}
@@ -88,13 +90,20 @@ def tile_kktloss_pc_t_kernel(
             held[c] = chunk
 
         def load_step(c):
-            load_chunk(gens, pq_pool, "gens_chunk", gens_rows, c, pieces=2 if c == ROUNDS - 1 else 1)
+            load_chunk(gens, pq_pool, "gens_chunk", gens_rows, c)
             if c + VOLT_AHEAD < ROUNDS:
                 load_chunk(volt, volt_pool, "volt_chunk", volt_rows, c + VOLT_AHEAD)
-            if c + 1 < ROUNDS:
-                load_chunk(
-                    loads, pq_pool, "loads_chunk", loads_rows, c + 1, pieces=1
-                )
+            load_chunk(loads, pq_pool, "loads_chunk", loads_rows, c + 1)
+
+        def load_last():
+            load_chunk(loads, pq_pool, "loads_chunk", loads_rows, ROUNDS - 1)
+            last = pq_pool.tile([P, ROUND_TILES, K], BF16, name="gens_chunk")
+            gens[ROUNDS - 1] = last
+            half = ROUND_TILES // 2
+            first = (ROUNDS - 1) * ROUND_TILES
+            nc.sync.dma_start(out=last[:, 0:half, :], in_=gens_rows[:, first : first + half, :])
+            load_chunk(gens, pq_pool, "gens_chunk", gens_rows, ROUNDS - 2)
+            nc.sync.dma_start(out=last[:, half:, :], in_=gens_rows[:, first + half :, :])
 
         def load_scales(w, scales):
             by_row = scales.bitcast(I32).rearrange("g (q r) n -> r q g n", r=4)
@@ -179,16 +188,16 @@ def tile_kktloss_pc_t_kernel(
                 out=copied[:], in_=row_tile(chunks, i), func=COPY, scale=sign, accum_out=sums[:, i : i + 1]
             )
 
-        def gens_on_vector(i):
-            negated = unread_pool.tile([P, K], BF16, name="negated")
+        def sum_on_vector(chunks, i, sign, sums):
+            signed = unread_pool.tile([P, K], BF16, name="signed")
             nc.vector.tensor_scalar(
-                out=negated[:],
-                in0=row_tile(gens, i),
-                scalar1=-1.0,
+                out=signed[:],
+                in0=row_tile(chunks, i),
+                scalar1=sign,
                 scalar2=None,
                 op0=MULT,
                 op1=ADD,
-                accum_out=gen_sums[:, i : i + 1],
+                accum_out=sums[:, i : i + 1],
             )
 
         def subtract_on_gpsimd(i):
@@ -223,43 +232,73 @@ def tile_kktloss_pc_t_kernel(
             tiles = range(r * ROUND_TILES, (r + 1) * ROUND_TILES)
             ahead = (r + VOLT_AHEAD) * ROUND_TILES
             prepared = range(min(ahead, TILES), min(ahead + ROUND_TILES, TILES))
-            by = {who: [i for i, w in zip(tiles, BALANCE[r]) if w == who] for who in "VSXG"}
-            if r + LOADS_AHEAD < ROUNDS:
+            by = {who: [i for i, w in zip(tiles, BALANCE[r]) if w == who] for who in "VSTG"}
+            if r + LOADS_AHEAD < ROUNDS - 2:
                 load_step(r + LOADS_AHEAD)
+            elif r + LOADS_AHEAD == ROUNDS - 2:
+                load_last()
 
             for i in tiles:
                 multiply(i)
             for i in prepared:
                 transpose(i)
 
-            for i in by["G"]:
-                subtract_on_gpsimd(i)
+            if r == ROUNDS - 1:
+                nc.gpsimd.tensor_copy(out=seen[:], in_=codes[TILES - 1][:, 0, 0:1])
+                for i in by["G"]:
+                    subtract_on_gpsimd(i)
 
-            for i in tiles:
-                if i in by["S"] or i in by["X"]:
+            if r < ROUNDS - 2:
+                for i in by["S"]:
                     sum_on_scalar(loads, i, 1.0, balance)
-            for i in by["S"]:
-                sum_on_scalar(gens, i, -1.0, gen_sums)
-            for i in by["G"]:
-                difference_on_scalar(i)
+                for i in by["S"]:
+                    sum_on_scalar(gens, i, -1.0, gen_sums)
+            elif r == ROUNDS - 2:
+                late = by
+                for i in by["S"]:
+                    sum_on_scalar(loads, i, 1.0, balance)
+            else:
+                for i in by["S"]:
+                    sum_on_scalar(loads, i, 1.0, balance)
+                for i in by["S"]:
+                    sum_on_scalar(gens, i, -1.0, gen_sums)
+                for i in late["S"]:
+                    sum_on_scalar(gens, i, -1.0, gen_sums)
+                for i in by["G"]:
+                    difference_on_scalar(i)
             for i in prepared:
                 regroup(i)
 
-            sums = [(balance_on_vector, i) for i in by["V"]] + [(gens_on_vector, i) for i in by["X"]]
-            if r == ROUNDS - 1:
-                for work, i in sums:
-                    work(i)
-                for i in tiles:
-                    dot(i)
-            else:
+            if r < ROUNDS - 2:
                 for j, i in enumerate(tiles):
                     dot(i)
                     if j == 0:
-                        for work, tile in sums:
-                            work(tile)
-            for i in prepared:
-                quantise(i)
+                        for b in by["V"]:
+                            balance_on_vector(b)
+                nxt = [i for i, w in zip(range(tiles.stop, tiles.stop + ROUND_TILES), BALANCE[r + 1]) if w == "T"]
+                for j, i in enumerate(prepared):
+                    quantise(i)
+                    if j % 2 == 0 and nxt:
+                        sum_on_vector(loads, nxt.pop(0), 1.0, balance)
+            elif r == ROUNDS - 2:
+                lasts = [tiles.stop + j for j, w in enumerate(BALANCE[r + 1]) if w == "T"]
+                for j, i in enumerate(tiles):
+                    dot(i)
+                    if j == 0:
+                        for t in lasts:
+                            sum_on_vector(loads, t, 1.0, balance)
+            else:
+                work = late["T"] + by["T"]
+                for j, i in enumerate(tiles):
+                    if j < len(work):
+                        sum_on_vector(gens, work[j], -1.0, gen_sums)
+                    dot(i)
 
-        nc.vector.tensor_tensor(out=balance[:], in0=balance[:], in1=gen_sums[:], op=ADD)
-        nc.vector.tensor_tensor(out=total[:], in0=dots[:], in1=balance[:], op=ADD)
+        for columns in (slice(0, TILES - ROUND_TILES), slice(TILES - ROUND_TILES, TILES)):
+            nc.vector.tensor_reduce(
+                out=total[:, columns],
+                in_=parts[:, :, columns].rearrange("p part t -> p t part"),
+                op=ADD,
+                axis=mybir.AxisListType.X,
+            )
         nc.sync.dma_start(out=out_rows, in_=total[:])

@@ -31,7 +31,7 @@ LOADS_AHEAD = 2
 VOLT_AHEAD = 2
 PQ_BUFS = 5
 
-BALANCE = ["VSVS"] * (ROUNDS - 2) + ["TSTS", "SGTG"]
+BALANCE = ["XSXS"] + ["VSVS"] * (ROUNDS - 3) + ["TSTS", "SGTG"]
 
 
 def tile_kktloss_pc_t_kernel(
@@ -50,7 +50,7 @@ def tile_kktloss_pc_t_kernel(
         pq_pool = stack.enter_context(tc.tile_pool(name="pq", bufs=PQ_BUFS))
         grouped_pool = stack.enter_context(tc.tile_pool(name="grouped", bufs=2 * ROUND_TILES))
         codes_pool = stack.enter_context(tc.tile_pool(name="codes", bufs=3 * ROUND_TILES))
-        difference_pool = stack.enter_context(tc.tile_pool(name="difference", bufs=2))
+        difference_pool = stack.enter_context(tc.tile_pool(name="difference", bufs=3))
         unread_pool = stack.enter_context(tc.tile_pool(name="unread", bufs=3))
         turned_pool = stack.enter_context(tc.psum_pool(name="turned", bufs=4))
         acc_pool = stack.enter_context(tc.psum_pool(name="acc", bufs=4))
@@ -90,9 +90,9 @@ def tile_kktloss_pc_t_kernel(
             held[c] = chunk
 
         def load_step(c):
-            load_chunk(gens, pq_pool, "gens_chunk", gens_rows, c)
             if c + VOLT_AHEAD < ROUNDS:
                 load_chunk(volt, volt_pool, "volt_chunk", volt_rows, c + VOLT_AHEAD)
+            load_chunk(gens, pq_pool, "gens_chunk", gens_rows, c)
             load_chunk(loads, pq_pool, "loads_chunk", loads_rows, c + 1)
 
         def load_last():
@@ -232,7 +232,7 @@ def tile_kktloss_pc_t_kernel(
             tiles = range(r * ROUND_TILES, (r + 1) * ROUND_TILES)
             ahead = (r + VOLT_AHEAD) * ROUND_TILES
             prepared = range(min(ahead, TILES), min(ahead + ROUND_TILES, TILES))
-            by = {who: [i for i, w in zip(tiles, BALANCE[r]) if w == who] for who in "VSTG"}
+            by = {who: [i for i, w in zip(tiles, BALANCE[r]) if w == who] for who in "VSXTG"}
             if r + LOADS_AHEAD < ROUNDS - 2:
                 load_step(r + LOADS_AHEAD)
             elif r + LOADS_AHEAD == ROUNDS - 2:
@@ -249,8 +249,11 @@ def tile_kktloss_pc_t_kernel(
                     subtract_on_gpsimd(i)
 
             if r < ROUNDS - 2:
-                for i in by["S"]:
-                    sum_on_scalar(loads, i, 1.0, balance)
+                for i in tiles:
+                    if i in by["S"] or i in by["X"]:
+                        sum_on_scalar(loads, i, 1.0, balance)
+                for i in prepared:
+                    regroup(i)
                 for i in by["S"]:
                     sum_on_scalar(gens, i, -1.0, gen_sums)
             elif r == ROUNDS - 2:
@@ -266,15 +269,14 @@ def tile_kktloss_pc_t_kernel(
                     sum_on_scalar(gens, i, -1.0, gen_sums)
                 for i in by["G"]:
                     difference_on_scalar(i)
-            for i in prepared:
-                regroup(i)
 
             if r < ROUNDS - 2:
-                for j, i in enumerate(tiles):
+                for i in tiles:
                     dot(i)
-                    if j == 0:
-                        for b in by["V"]:
-                            balance_on_vector(b)
+                for b in by["V"]:
+                    balance_on_vector(b)
+                for b in by["X"]:
+                    sum_on_vector(gens, b, -1.0, gen_sums)
                 nxt = [i for i, w in zip(range(tiles.stop, tiles.stop + ROUND_TILES), BALANCE[r + 1]) if w == "T"]
                 for j, i in enumerate(prepared):
                     quantise(i)

from contextlib import ExitStack

import concourse.mybir as mybir
from concourse.masks import make_identity

FLOPS = 2 * 2 * 4096 * 1024 * 512

BF16 = mybir.dt.bfloat16
F32 = mybir.dt.float32
I32 = mybir.dt.int32
U32 = mybir.dt.uint32
U8 = mybir.dt.uint8
FP8X4 = mybir.dt.float8_e4m3fn_x4
FP4X4 = mybir.dt.float4_e2m1fn_x4
MULT = mybir.AluOpType.mult
ADD = mybir.AluOpType.add
SUBTRACT = mybir.AluOpType.subtract
COPY = mybir.ActivationFunctionType.Copy

P = 128
BATCH = 4096
K = 1024
NB = 512
K_PASS = 512
GROUPS = K // K_PASS
WEIGHTS = 2
TILES = BATCH // P
ROUND_TILES = 4
ROUNDS = TILES // ROUND_TILES
LOADS_AHEAD = 2
VOLT_AHEAD = 2
PQ_BUFS = 5

BALANCE = ["XSXS"] + ["VSVS"] * (ROUNDS - 3) + ["TSTS", "SGTG"]


def tile_kktloss_pc_t_kernel(
    tc, Volt, Y_top_words, Y_top_scales, Yconj_top_words, Yconj_top_scales, PQ_Loads, PQ_Gens, out
):
    nc = tc.nc

    volt_rows = Volt.rearrange("(p t) k -> p t k", t=TILES)
    loads_rows = PQ_Loads.rearrange("(p t) k -> p t k", t=TILES)
    gens_rows = PQ_Gens.rearrange("(p t) k -> p t k", t=TILES)
    out_rows = out.rearrange("(p t) -> p t", t=TILES)

    with ExitStack() as stack:
        const = stack.enter_context(tc.tile_pool(name="const", bufs=1))
        volt_pool = stack.enter_context(tc.tile_pool(name="volt", bufs=ROUNDS))
        pq_pool = stack.enter_context(tc.tile_pool(name="pq", bufs=PQ_BUFS))
        grouped_pool = stack.enter_context(tc.tile_pool(name="grouped", bufs=2 * ROUND_TILES))
        codes_pool = stack.enter_context(tc.tile_pool(name="codes", bufs=3 * ROUND_TILES))
        difference_pool = stack.enter_context(tc.tile_pool(name="difference", bufs=3))
        unread_pool = stack.enter_context(tc.tile_pool(name="unread", bufs=3))
        turned_pool = stack.enter_context(tc.psum_pool(name="turned", bufs=4))
        acc_pool = stack.enter_context(tc.psum_pool(name="acc", bufs=4))
        stack.enter_context(tc.manual_schedule())

        identity = const.tile([P, P], F32)
        make_identity(nc, identity[:])

        w_words = const.tile([P, WEIGHTS, GROUPS, 2 * NB], U8, align_bytes=64)
        w_planes = const.tile([P, WEIGHTS, GROUPS, NB], U8, align_bytes=64)
        nc.vector.memset(w_planes[:].rearrange("p w g n -> p (w g n)").bitcast(I32), 0)

        parts = const.tile([P, 3, TILES], F32)
        dots = parts[:, 0, :]
        balance = parts[:, 1, :]
        gen_sums = parts[:, 2, :]
        nc.gpsimd.memset(gen_sums, 0.0)
        total = const.tile([P, TILES], F32)
        seen = const.tile([P, 1], U32)

        volt = {}
        loads = {}
        gens = {}
        turned = {}
        grouped = {}
        subtracted = {}
        codes = {}
        code_scales = {}
        acc = {}

        def load_chunk(held, pool, name, rows, c, pieces=1):
            chunk = pool.tile([P, ROUND_TILES, K], BF16, name=name)
            step = ROUND_TILES // pieces
            for s in range(0, ROUND_TILES, step):
                first = c * ROUND_TILES + s
                nc.sync.dma_start(out=chunk[:, s : s + step, :], in_=rows[:, first : first + step, :])
            held[c] = chunk

        def load_step(c):
            if c + VOLT_AHEAD < ROUNDS:
                load_chunk(volt, volt_pool, "volt_chunk", volt_rows, c + VOLT_AHEAD)
            load_chunk(gens, pq_pool, "gens_chunk", gens_rows, c)
            load_chunk(loads, pq_pool, "loads_chunk", loads_rows, c + 1)

        def load_last():
            load_chunk(loads, pq_pool, "loads_chunk", loads_rows, ROUNDS - 1)
            last = pq_pool.tile([P, ROUND_TILES, K], BF16, name="gens_chunk")
            gens[ROUNDS - 1] = last
            half = ROUND_TILES // 2
            first = (ROUNDS - 1) * ROUND_TILES
            nc.sync.dma_start(out=last[:, 0:half, :], in_=gens_rows[:, first : first + half, :])
            load_chunk(gens, pq_pool, "gens_chunk", gens_rows, ROUNDS - 2)
            nc.sync.dma_start(out=last[:, half:, :], in_=gens_rows[:, first + half :, :])

        def load_scales(w, scales):
            by_row = scales.bitcast(I32).rearrange("g (q r) n -> r q g n", r=4)
            for r in range(4):
                nc.sync.dma_start(out=w_planes[r:P:32, w].bitcast(I32), in_=by_row[r])

        def load_words(w, words):
            nc.sync.dma_start(out=w_words[:, w].bitcast(I32), in_=words.bitcast(I32).rearrange("g p n -> p g n"))

        def row_tile(chunks, i):
            return chunks[i // ROUND_TILES][:, i % ROUND_TILES, :]

        def transpose(i):
            words = row_tile(volt, i).bitcast(F32)
            bank = turned_pool.tile([P, GROUPS, 2, P], F32, name="turned_bank")
            for g in range(GROUPS):
                for u in range(2):
                    nc.tensor.transpose(bank[:, g, u, :], words[:, 256 * g + u : 256 * (g + 1) : 2], identity[:])
            turned[i] = bank

        def regroup(i):
            side_by_side = grouped_pool.tile([P, K], BF16, name="side_by_side", align_bytes=64)
            nc.scalar.copy(
                out=side_by_side[:].bitcast(F32).rearrange("p (g b u) -> p g b u", g=GROUPS, u=2),
                in_=turned[i][:].rearrange("p g u b -> p g b u"),
            )
            grouped[i] = side_by_side

        def quantise(i):
            packed = codes_pool.tile([P, GROUPS, P], U32, name="packed", align_bytes=64)
            plane = codes_pool.tile([P, GROUPS, P], U8, name="plane", align_bytes=64)
            nc.vector.quantize_mx(
                out=packed[:].rearrange("p g b -> p (g b)").bitcast(FP8X4),
                scales=plane[:].rearrange("p g b -> p (g b)"),
                in_=grouped[i][:],
            )
            codes[i] = packed
            code_scales[i] = plane

        def multiply(i):
            bank = acc_pool.tile([P, NB], F32, name="acc_bank")
            for g in range(GROUPS):
                for w in range(WEIGHTS):
                    nc.tensor.matmul_mx(
                        out=bank[:],
                        lhsT=codes[i][:, g, :].bitcast(FP8X4),
                        lhsT_scale=code_scales[i][:, g, :],
                        rhs=w_words[:, w, g, :].bitcast(FP4X4),
                        rhs_scale=w_planes[:, w, g, :],
                        start=(g == 0 and w == 0),
                        stop=(g == GROUPS - 1 and w == WEIGHTS - 1),
                    )
            acc[i] = bank

        def dot(i):
            products = unread_pool.tile([P, NB], F32, name="products")
            nc.vector.scalar_tensor_tensor(
                out=products[:],
                in0=acc[i][:],
                scalar=1.0,
                in1=row_tile(volt, i)[:, 0:NB],
                op0=MULT,
                op1=MULT,
                accum_out=dots[:, i : i + 1],
            )

        def balance_on_vector(i):
            differences = unread_pool.tile([P, K], BF16, name="differences")
            nc.vector.scalar_tensor_tensor(
                out=differences[:],
                in0=row_tile(loads, i),
                scalar=1.0,
                in1=row_tile(gens, i),
                op0=MULT,
                op1=SUBTRACT,
                accum_out=balance[:, i : i + 1],
            )

        def sum_on_scalar(chunks, i, sign, sums):
            copied = unread_pool.tile([P, K], BF16, name="copied")
            nc.scalar.activation(
                out=copied[:], in_=row_tile(chunks, i), func=COPY, scale=sign, accum_out=sums[:, i : i + 1]
            )

        def sum_on_vector(chunks, i, sign, sums):
            signed = unread_pool.tile([P, K], BF16, name="signed")
            nc.vector.tensor_scalar(
                out=signed[:],
                in0=row_tile(chunks, i),
                scalar1=sign,
                scalar2=None,
                op0=MULT,
                op1=ADD,
                accum_out=sums[:, i : i + 1],
            )

        def subtract_on_gpsimd(i):
            difference = difference_pool.tile([P, K], F32, name="difference")
            for h in range(0, K, K // 2):
                half = slice(h, h + K // 2)
                nc.gpsimd.tensor_tensor(
                    out=difference[:, half], in0=row_tile(loads, i)[:, half], in1=row_tile(gens, i)[:, half], op=SUBTRACT
                )
            subtracted[i] = difference

        def difference_on_scalar(i):
            copied = unread_pool.tile([P, K], BF16, name="copied")
            nc.scalar.activation(out=copied[:], in_=subtracted[i][:], func=COPY, accum_out=balance[:, i : i + 1])

        load_chunk(volt, volt_pool, "volt_chunk", volt_rows, 0)
        load_scales(0, Y_top_scales)
        load_words(0, Y_top_words)
        load_chunk(volt, volt_pool, "volt_chunk", volt_rows, 1)
        load_scales(1, Yconj_top_scales)
        load_words(1, Yconj_top_words)
        load_chunk(loads, pq_pool, "loads_chunk", loads_rows, 0)
        for c in range(LOADS_AHEAD):
            load_step(c)

        for i in range(VOLT_AHEAD * ROUND_TILES):
            transpose(i)
            regroup(i)
            quantise(i)

        for r in range(ROUNDS):
            tiles = range(r * ROUND_TILES, (r + 1) * ROUND_TILES)
            ahead = (r + VOLT_AHEAD) * ROUND_TILES
            prepared = range(min(ahead, TILES), min(ahead + ROUND_TILES, TILES))
            by = {who: [i for i, w in zip(tiles, BALANCE[r]) if w == who] for who in "VSXTG"}
            if r + LOADS_AHEAD < ROUNDS - 2:
                load_step(r + LOADS_AHEAD)
            elif r + LOADS_AHEAD == ROUNDS - 2:
                load_last()

            for i in tiles:
                multiply(i)
            for i in prepared:
                transpose(i)

            if r == ROUNDS - 1:
                nc.gpsimd.tensor_copy(out=seen[:], in_=codes[TILES - 1][:, 0, 0:1])
                for i in by["G"]:
                    subtract_on_gpsimd(i)

            if r < ROUNDS - 2:
                for i in tiles:
                    if i in by["S"] or i in by["X"]:
                        sum_on_scalar(loads, i, 1.0, balance)
                for i in prepared:
                    regroup(i)
                for i in by["S"]:
                    sum_on_scalar(gens, i, -1.0, gen_sums)
            elif r == ROUNDS - 2:
                late = by
                for i in by["S"]:
                    sum_on_scalar(loads, i, 1.0, balance)
            else:
                for i in by["S"]:
                    sum_on_scalar(loads, i, 1.0, balance)
                for i in by["S"]:
                    sum_on_scalar(gens, i, -1.0, gen_sums)
                for i in late["S"]:
                    sum_on_scalar(gens, i, -1.0, gen_sums)
                for i in by["G"]:
                    difference_on_scalar(i)

            if r < ROUNDS - 2:
                for i in tiles:
                    dot(i)
                for b in by["V"]:
                    balance_on_vector(b)
                for b in by["X"]:
                    sum_on_vector(gens, b, -1.0, gen_sums)
                nxt = [i for i, w in zip(range(tiles.stop, tiles.stop + ROUND_TILES), BALANCE[r + 1]) if w == "T"]
                for j, i in enumerate(prepared):
                    quantise(i)
                    if j % 2 == 0 and nxt:
                        sum_on_vector(loads, nxt.pop(0), 1.0, balance)
            elif r == ROUNDS - 2:
                lasts = [tiles.stop + j for j, w in enumerate(BALANCE[r + 1]) if w == "T"]
                for j, i in enumerate(tiles):
                    dot(i)
                    if j == 0:
                        for t in lasts:
                            sum_on_vector(loads, t, 1.0, balance)
            else:
                work = late["T"] + by["T"]
                for j, i in enumerate(tiles):
                    if j < len(work):
                        sum_on_vector(gens, work[j], -1.0, gen_sums)
                    dot(i)

        for columns in (slice(0, TILES - ROUND_TILES), slice(TILES - ROUND_TILES, TILES)):
            nc.vector.tensor_reduce(
                out=total[:, columns],
                in_=parts[:, :, columns].rearrange("p part t -> p t part"),
                op=ADD,
                axis=mybir.AxisListType.X,
            )
        nc.sync.dma_start(out=out_rows, in_=total[:])
